import numpy as np
import ml_dtypes


def mxq(x, axis, fmt="e4m3"):
    dtype, down = {"e4m3": (ml_dtypes.float8_e4m3fn, 7), "e5m2": (ml_dtypes.float8_e5m2, 14)}[fmt]
    v = np.moveaxis(np.asarray(x, np.float32).astype(ml_dtypes.bfloat16).astype(np.float64), axis, -1)
    blocks = v.reshape(v.shape[:-1] + (-1, 32))
    amax = np.abs(blocks).max(-1, keepdims=True)
    byte = np.maximum(np.where(amax > 0, np.frexp(amax)[1] - 1 + 127, 0) - down, 1)
    scale = np.exp2(byte - 127.0)
    codes = (blocks / scale).astype(np.float32).astype(dtype).astype(np.float64)
    return np.moveaxis((codes * scale).reshape(v.shape), -1, axis)


WIDE = False


def mx_kscale(k):
    if not WIDE:
        return np.ones(k)
    levels = np.array([10, -10, 5, -5, 0])
    a = np.random.permutation(np.resize(levels, k // 512 * 4)).reshape(k // 512, 4)
    idx = np.arange(k)
    return np.exp2(a[idx // 512, idx % 128 // 32])


BF16 = ml_dtypes.bfloat16


def bf(x):
    return np.asarray(x, np.float32).astype(BF16)


def f64(x):
    return np.asarray(x).astype(np.float64)


B, DETER, STOCH, ACT, HID, BLOCKS, NIN, NG = 4096, 512, 1024, 512, 512, 1, 3, 3
DPB = DETER // BLOCKS
EPS = 1e-4


def silu(v):
    return v / (1.0 + np.exp(-v))


def sigmoid(v):
    return 1.0 / (1.0 + np.exp(-v))


def rmsnorm(v, g):
    return v * (1.0 / np.sqrt(np.mean(v * v, axis=-1, keepdims=True) + EPS)) * g


def setup_inputs():
    s = mx_kscale(DETER)
    n = np.random.standard_normal
    return {"hid0": bf(silu(n((B, DETER))) * s), "deter": bf(n((B, DETER))),
            "hw1": bf(n((BLOCKS, DPB, DPB)) * 1.5 / np.sqrt(DPB) / s.reshape(BLOCKS, DPB, 1)), "hb1": bf(n(DETER) * 0.1), "hg1": bf(1.0 + n(DETER) * 0.1),
            "gw": bf(n((BLOCKS, DPB, NG * DPB)) * 2.0 / np.sqrt(DPB)), "gb": bf(n(NG * DETER) * 0.2)}


def block_linear(vq, wq, b):
    y = vq.transpose(1, 0, 2) @ wq
    return y.transpose(1, 0, 2).reshape(B, -1) + b


def reference(hid0, deter, hw1, hb1, hg1, gw, gb):
    u = block_linear(mxq(f64(hid0).reshape(B, BLOCKS, DPB), 2, "e4m3"), mxq(f64(hw1), 1, "e4m3"), f64(hb1))
    h = silu(rmsnorm(u, f64(hg1)))
    p = block_linear(mxq(h.reshape(B, BLOCKS, DPB), 2, "e4m3"), mxq(f64(gw), 1, "e4m3"), f64(gb))
    g = p.reshape(B, BLOCKS, NG, DPB)
    reset = sigmoid(g[:, :, 0, :].reshape(B, DETER))
    cand = np.tanh(reset * g[:, :, 1, :].reshape(B, DETER))
    update = sigmoid(g[:, :, 2, :].reshape(B, DETER) - 1.0)
    return update * cand + (1.0 - update) * f64(deter)

@@ -1,0 +1,365 @@
+import concourse.mybir as mybir
+from concourse.masks import make_identity
+
+F32 = mybir.dt.float32
+BF16 = mybir.dt.bfloat16
+U32 = mybir.dt.uint32
+U8 = mybir.dt.uint8
+FP8X4 = mybir.dt.float8_e4m3fn_x4
+ACT = mybir.ActivationFunctionType
+ALU = mybir.AluOpType
+
+P = 128
+PACK = 4
+BATCH = 4096
+WIDTH = 512
+GATES = 3
+EPS = 1e-4
+CHUNK = 512
+ROW_TILES = CHUNK // P
+COL_TILES = WIDTH // P
+N_CHUNKS = BATCH // CHUNK
+N_ROW_TILES = BATCH // P
+N_UNITS = N_CHUNKS * COL_TILES
+LAG = 6
+QUANT_COLS = 512
+
+FLOPS = 2 * BATCH * WIDTH * (WIDTH + GATES * WIDTH)
+
+
+def quantise_weight(nc, stage, raw, codes, scales, piece):
+    cols = slice(piece * QUANT_COLS, (piece + 1) * QUANT_COLS)
+    grouped = stage.tile([P, QUANT_COLS, PACK], BF16, align_bytes=64)
+    nc.vector.tensor_copy(
+        out=grouped[:].rearrange("p (c i) t -> p c t i", i=4),
+        in_=raw[:, :, cols].rearrange("p t (c i) -> p c t i", i=4),
+    )
+    nc.vector.quantize_mx(
+        out=codes[:, cols].bitcast(FP8X4),
+        scales=scales[:, cols],
+        in_=grouped[:].rearrange("p c t -> p (c t)"),
+    )
+
+
+def tile_deter_pb_t_kernel(tc, hid0, deter, hw1, hb1, hg1, gw, gb, out):
+    nc = tc.nc
+    hw1_rows = hw1.rearrange("o k f -> (o k) f")
+    gw_rows = gw.rearrange("o k n -> (o k) n")
+
+    def chunk_view(dram, c):
+        return dram[c * CHUNK : (c + 1) * CHUNK, :].rearrange("(p j) f -> p j f", j=ROW_TILES)
+
+    with tc.tile_pool(name="const", bufs=1) as const, tc.tile_pool(
+        name="stage", bufs=2
+    ) as stage, tc.tile_pool(name="work", bufs=3) as work, tc.manual_schedule():
+        hw_raw = const.tile([P, PACK, WIDTH], BF16)
+        for u in range(2):
+            nc.sync.dma_start(
+                out=hw_raw[:, 2 * u : 2 * u + 2, :],
+                in_=hw1_rows[256 * u : 256 * (u + 1), :].rearrange("(q e) c -> q e c", e=2),
+            )
+        x_chunks = []
+        for c in range(N_CHUNKS):
+            x_rows = const.tile([P, ROW_TILES, WIDTH], BF16, name="x_rows%d" % c)
+            x_chunks.append(x_rows)
+        nc.sync.dma_start(out=x_chunks[0][:], in_=chunk_view(hid0, 0))
+        nc.sync.dma_start(out=x_chunks[1][:], in_=chunk_view(hid0, 1))
+        gw_raw = const.tile([P, PACK, GATES * WIDTH], BF16)
+        nc.sync.dma_start(out=gw_raw[:], in_=gw_rows.rearrange("(t p) n -> p t n", p=P))
+        for c in range(2, N_CHUNKS):
+            nc.sync.dma_start(out=x_chunks[c][:], in_=chunk_view(hid0, c))
+        d_chunks = []
+        for c in range(N_CHUNKS):
+            d_rows = const.tile([P, ROW_TILES, WIDTH], BF16, name="d_rows%d" % c)
+            nc.sync.dma_start(out=d_rows[:], in_=chunk_view(deter, c))
+            d_chunks.append(d_rows)
+
+        gb_rows = const.tile([P, P], BF16)
+        nc.vector.memset(gb_rows[:], 0.0)
+        nc.scalar.dma_start(
+            out=gb_rows[0 : GATES * COL_TILES, :], in_=gb.rearrange("(r c) -> r c", c=P)
+        )
+        hb_all = const.tile([P, WIDTH], BF16)
+        hg_all = const.tile([P, WIDTH], BF16)
+        nc.scalar.dma_start(out=hb_all[:], in_=hb1.partition_broadcast(P))
+        nc.scalar.dma_start(out=hg_all[:], in_=hg1.partition_broadcast(P))
+
+        minus_half = const.tile([P, ROW_TILES], F32)
+        nc.vector.memset(minus_half[:], -0.5)
+        warm = const.tile([P, 1], F32)
+        nc.scalar.activation(out=warm[:], in_=minus_half[:, 0:1], func=ACT.Silu)
+        ident_f32 = const.tile([P, P], F32)
+        make_identity(nc, ident_f32[:])
+        ident_bf16 = const.tile([P, P], BF16)
+        make_identity(nc, ident_bf16[:])
+
+        hw_codes = const.tile([P, WIDTH], U32, align_bytes=64)
+        hw_scales = const.tile([P, WIDTH], U8, align_bytes=64)
+        quantise_weight(nc, stage, hw_raw, hw_codes, hw_scales, 0)
+        gw_codes = const.tile([P, GATES * WIDTH], U32, align_bytes=64)
+        gw_scales = const.tile([P, GATES * WIDTH], U8, align_bytes=64)
+
+        h_codes = const.tile([P, BATCH], U32, align_bytes=64)
+        h_scales = const.tile([P, BATCH], U8, align_bytes=64)
+
+        with tc.psum_pool(name="psum_one", bufs=3) as psum:
+            gb_t = psum.tile([P, P], BF16, tag="x_t", bufs=2)
+            nc.tensor.transpose(gb_t[:], gb_rows[:], ident_bf16[:])
+            gate_bias = const.tile([P, GATES * COL_TILES], F32)
+            nc.vector.tensor_copy(out=gate_bias[:], in_=gb_t[:, 0 : GATES * COL_TILES])
+            z_bias = gate_bias[:, 2 * COL_TILES : 3 * COL_TILES]
+            nc.vector.tensor_scalar_add(out=z_bias, in0=z_bias, scalar1=-1.0)
+
+            x_banks = {}
+            x_grouped_of = {}
+            x_packed = {}
+            sum_sq_of = {}
+            inv_rms_of = {}
+            gained = {}
+            h_grouped_of = {}
+
+            def transpose_x(c):
+                x_banks[c] = []
+                for pair in range(ROW_TILES // 2):
+                    x_t = psum.tile([P, 2, 2, P], F32, tag="x_t", bufs=2)
+                    for jj in range(2):
+                        for u in range(2):
+                            nc.tensor.transpose(
+                                x_t[:, jj, u, :],
+                                x_chunks[c][:, 2 * pair + jj, :].bitcast(F32)[:, u * P : (u + 1) * P],
+                                ident_f32[:],
+                            )
+                    x_banks[c].append(x_t)
+
+            def copy_x(c):
+                x_grouped = stage.tile([P, CHUNK * PACK], BF16, align_bytes=64)
+                x_words = x_grouped[:].bitcast(F32).rearrange(
+                    "p (j b u) -> p j b u", j=ROW_TILES, u=2
+                )
+                for pair in range(ROW_TILES // 2):
+                    nc.scalar.copy(
+                        out=x_words[:, 2 * pair : 2 * pair + 2],
+                        in_=x_banks[c][pair][:].rearrange("p j u b -> p j b u"),
+                    )
+                x_grouped_of[c] = x_grouped
+
+            def quantise_x(c):
+                x_codes = stage.tile([P, CHUNK], U32, align_bytes=64)
+                x_scales = stage.tile([P, CHUNK], U8, align_bytes=64)
+                nc.vector.quantize_mx(
+                    out=x_codes[:].bitcast(FP8X4), scales=x_scales[:], in_=x_grouped_of[c][:]
+                )
+                x_packed[c] = (x_codes, x_scales)
+
+            def product(i):
+                c, j = divmod(i, ROW_TILES)
+                x_codes, x_scales = x_packed[c]
+                rows = slice(j * P, (j + 1) * P)
+                u_ps = psum.tile([P, WIDTH], F32)
+                nc.tensor.matmul_mx(
+                    out=u_ps[:],
+                    lhsT=x_codes[:, rows].bitcast(FP8X4),
+                    lhsT_scale=x_scales[:, rows],
+                    rhs=hw_codes[:].bitcast(FP8X4),
+                    rhs_scale=hw_scales[:],
+                    start=True,
+                    stop=True,
+                )
+                u_sb = work.tile([P, WIDTH], F32, bufs=4)
+                nc.vector.tensor_tensor(out=u_sb[:], in0=u_ps[:], in1=hb_all[:], op=ALU.add)
+                return u_sb
+
+            def squares_and_gain(i, u_sb):
+                c, j = divmod(i, ROW_TILES)
+                if j == 0:
+                    sum_sq = work.tile([P, ROW_TILES], F32)
+                    sum_sq_of[c] = sum_sq
+                squares = work.tile([P, WIDTH], BF16)
+                nc.scalar.activation(
+                    out=squares[:], in_=u_sb[:], func=ACT.Square,
+                    accum_out=sum_sq_of[c][:, j : j + 1],
+                )
+                u_gain = work.tile([P, WIDTH], F32, bufs=LAG + 2)
+                nc.gpsimd.tensor_tensor(out=u_gain[:], in0=u_sb[:], in1=hg_all[:], op=ALU.mult)
+                gained[i] = u_gain
+
+            def inverse_rms(c):
+                mean_sq = work.tile([P, ROW_TILES], F32)
+                nc.gpsimd.tensor_scalar(
+                    out=mean_sq[:], in0=sum_sq_of[c][:], scalar1=1.0 / WIDTH, scalar2=EPS,
+                    op0=ALU.mult, op1=ALU.add,
+                )
+                inv_rms = work.tile([P, ROW_TILES], F32)
+                nc.gpsimd.tensor_tensor(
+                    out=inv_rms[:], in0=mean_sq[:], in1=minus_half[:], op=ALU.pow
+                )
+                inv_rms_of[c] = inv_rms
+
+            def normalise(i):
+                c, j = divmod(i, ROW_TILES)
+                normed = work.tile([P, WIDTH], F32)
+                nc.vector.tensor_scalar_mul(
+                    out=normed[:], in0=gained[i][:], scalar1=inv_rms_of[c][:, j : j + 1]
+                )
+                return normed
+
+            def transpose_and_silu(i, normed):
+                c, j = divmod(i, ROW_TILES)
+                if j == 0:
+                    h_grouped = stage.tile([P, ROW_TILES, P, PACK], BF16, align_bytes=64)
+                    h_grouped_of[c] = h_grouped
+                normed_t = psum.tile([P, COL_TILES, P], F32)
+                for t in range(COL_TILES):
+                    nc.tensor.transpose(
+                        normed_t[:, t, :], normed[:, t * P : (t + 1) * P], ident_f32[:]
+                    )
+                nc.scalar.activation(
+                    out=h_grouped_of[c][:, j, :, :],
+                    in_=normed_t[:].rearrange("p t b -> p b t"),
+                    func=ACT.Silu,
+                )
+
+            def quantise_h(c):
+                cols = slice(c * CHUNK, (c + 1) * CHUNK)
+                nc.vector.quantize_mx(
+                    out=h_codes[:, cols].bitcast(FP8X4),
+                    scales=h_scales[:, cols],
+                    in_=h_grouped_of[c][:].rearrange("p j b t -> p (j b t)"),
+                )
+
+            transpose_x(0)
+            copy_x(0)
+            quantise_x(0)
+            for i in range(N_ROW_TILES + LAG + 1):
+                c, j = divmod(i, ROW_TILES)
+                late = i - LAG
+                if 0 <= late < N_ROW_TILES:
+                    normed = normalise(late)
+                if i < N_ROW_TILES:
+                    if j == 0 and c + 1 < N_CHUNKS:
+                        transpose_x(c + 1)
+                    u_sb = product(i)
+                if 0 <= late < N_ROW_TILES:
+                    transpose_and_silu(late, normed)
+                if i < N_ROW_TILES:
+                    if j == 1 and c + 1 < N_CHUNKS:
+                        copy_x(c + 1)
+                    squares_and_gain(i, u_sb)
+                    if j == ROW_TILES - 1 and c + 1 < N_CHUNKS:
+                        quantise_x(c + 1)
+                if j == 0 and 1 <= c <= N_CHUNKS:
+                    inverse_rms(c - 1)
+                if late >= ROW_TILES and late % ROW_TILES == 0:
+                    quantise_h(late // ROW_TILES - 1)
+                if i < LAG and i % (LAG // GATES) == 1:
+                    quantise_weight(nc, stage, gw_raw, gw_codes, gw_scales, i // (LAG // GATES))
+
+        with tc.psum_pool(name="psum_two", bufs=1, reuse_waits="tile") as psum:
+            gate_banks = {}
+            deter_t = {}
+            resets, updates, cands, steps, moves = {}, {}, {}, {}, {}
+            out_rows_of = {}
+
+            def gate_products(n):
+                c, t = divmod(n, COL_TILES)
+                cols = slice(c * CHUNK, (c + 1) * CHUNK)
+                gate_banks[n] = []
+                for g in range(GATES):
+                    g_cols = slice(g * WIDTH + t * P, g * WIDTH + (t + 1) * P)
+                    g_ps = psum.tile([P, CHUNK], F32, bufs=2 * GATES)
+                    nc.tensor.matmul_mx(
+                        out=g_ps[:],
+                        lhsT=gw_codes[:, g_cols].bitcast(FP8X4),
+                        lhsT_scale=gw_scales[:, g_cols],
+                        rhs=h_codes[:, cols].bitcast(FP8X4),
+                        rhs_scale=h_scales[:, cols],
+                        start=True,
+                        stop=True,
+                    )
+                    gate_banks[n].append(g_ps)
+
+            def transpose_deter(n):
+                c, t = divmod(n, COL_TILES)
+                d_t = psum.tile([P, ROW_TILES, P], BF16)
+                for j in range(ROW_TILES):
+                    nc.tensor.transpose(
+                        d_t[:, j, :], d_chunks[c][:, j, t * P : (t + 1) * P], ident_bf16[:]
+                    )
+                deter_t[n] = d_t
+
+            def bias_of(g, n):
+                col = g * COL_TILES + n % COL_TILES
+                return gate_bias[:, col : col + 1]
+
+            def reset_and_update(n):
+                reset = work.tile([P, CHUNK], F32)
+                nc.scalar.activation(
+                    out=reset[:], in_=gate_banks[n][0][:], func=ACT.Sigmoid, bias=bias_of(0, n)
+                )
+                resets[n] = reset
+                update = work.tile([P, CHUNK], F32)
+                nc.scalar.activation(
+                    out=update[:], in_=gate_banks[n][2][:], func=ACT.Sigmoid, bias=bias_of(2, n)
+                )
+                updates[n] = update
+
+            def candidate(n):
+                gated = work.tile([P, CHUNK], F32)
+                nc.vector.scalar_tensor_tensor(
+                    out=gated[:], in0=gate_banks[n][1][:], scalar=bias_of(1, n), in1=resets[n][:],
+                    op0=ALU.add, op1=ALU.mult,
+                )
+                cand = work.tile([P, CHUNK], F32)
+                nc.scalar.activation(out=cand[:], in_=gated[:], func=ACT.Tanh)
+                cands[n] = cand
+
+            def step_towards_candidate(n):
+                step = work.tile([P, CHUNK], F32)
+                nc.vector.tensor_tensor(
+                    out=step[:], in0=cands[n][:], in1=deter_t[n][:].rearrange("p j b -> p (j b)"),
+                    op=ALU.subtract,
+                )
+                steps[n] = step
+
+            def scale_step(n):
+                move = work.tile([P, CHUNK], F32)
+                nc.gpsimd.tensor_tensor(out=move[:], in0=steps[n][:], in1=updates[n][:], op=ALU.mult)
+                moves[n] = move
+
+            def transpose_move(n):
+                move_t = psum.tile([P, ROW_TILES, P], F32)
+                for j in range(ROW_TILES):
+                    nc.tensor.transpose(
+                        move_t[:, j, :], moves[n][:, j * P : (j + 1) * P], ident_f32[:]
+                    )
+                return move_t
+
+            def finish(n, move_t):
+                c, t = divmod(n, COL_TILES)
+                feats = slice(t * P, (t + 1) * P)
+                if t == 0:
+                    out_rows = work.tile([P, ROW_TILES, WIDTH], F32, bufs=2)
+                    out_rows_of[c] = out_rows
+                nc.vector.tensor_tensor(
+                    out=out_rows_of[c][:, :, feats], in0=move_t[:], in1=d_chunks[c][:, :, feats],
+                    op=ALU.add,
+                )
+                if t == COL_TILES - 1:
+                    nc.sync.dma_start(out=chunk_view(out, c), in_=out_rows_of[c][:])
+
+            gate_products(0)
+            for n in range(N_UNITS + 2):
+                if 1 <= n <= N_UNITS:
+                    step_towards_candidate(n - 1)
+                if n >= 2:
+                    move_t = transpose_move(n - 2)
+                if n + 1 < N_UNITS:
+                    gate_products(n + 1)
+                if n < N_UNITS:
+                    transpose_deter(n)
+                    reset_and_update(n)
+                    candidate(n)
+                if 1 <= n <= N_UNITS:
+                    scale_step(n - 1)
+                if n >= 2:
+                    finish(n - 2, move_t)

@@ -21,7 +21,7 @@ COL_TILES = WIDTH // P
 N_CHUNKS = BATCH // CHUNK
 N_ROW_TILES = BATCH // P
 N_UNITS = N_CHUNKS * COL_TILES
-LAG = 6
+NORM_LAG = 8
 QUANT_COLS = 512
 
 FLOPS = 2 * BATCH * WIDTH * (WIDTH + GATES * WIDTH)
@@ -113,10 +113,19 @@ def tile_deter_pb_t_kernel(tc, hid0, deter, hw1, hb1, hg1, gw, gb, out):
             x_banks = {}
             x_grouped_of = {}
             x_packed = {}
+            products = {}
+            biased = {}
             sum_sq_of = {}
             inv_rms_of = {}
-            gained = {}
+            normed_of = {}
+            normed_t_of = {}
             h_grouped_of = {}
+
+            def is_chunk(c):
+                return 0 <= c < N_CHUNKS
+
+            def is_row_tile(i):
+                return 0 <= i < N_ROW_TILES
 
             def transpose_x(c):
                 x_banks[c] = []
@@ -165,23 +174,25 @@ def tile_deter_pb_t_kernel(tc, hid0, deter, hw1, hb1, hg1, gw, gb, out):
                     start=True,
                     stop=True,
                 )
-                u_sb = work.tile([P, WIDTH], F32, bufs=4)
-                nc.vector.tensor_tensor(out=u_sb[:], in0=u_ps[:], in1=hb_all[:], op=ALU.add)
-                return u_sb
+                products[i] = u_ps
 
-            def squares_and_gain(i, u_sb):
+            def add_bias(i):
+                u_sb = work.tile([P, WIDTH], F32, bufs=NORM_LAG + 1)
+                nc.vector.tensor_tensor(
+                    out=u_sb[:], in0=products[i][:], in1=hb_all[:], op=ALU.add
+                )
+                biased[i] = u_sb
+
+            def sum_squares(i):
                 c, j = divmod(i, ROW_TILES)
                 if j == 0:
                     sum_sq = work.tile([P, ROW_TILES], F32)
                     sum_sq_of[c] = sum_sq
                 squares = work.tile([P, WIDTH], BF16)
                 nc.scalar.activation(
-                    out=squares[:], in_=u_sb[:], func=ACT.Square,
+                    out=squares[:], in_=biased[i][:], func=ACT.Square,
                     accum_out=sum_sq_of[c][:, j : j + 1],
                 )
-                u_gain = work.tile([P, WIDTH], F32, bufs=LAG + 2)
-                nc.gpsimd.tensor_tensor(out=u_gain[:], in0=u_sb[:], in1=hg_all[:], op=ALU.mult)
-                gained[i] = u_gain
 
             def inverse_rms(c):
                 mean_sq = work.tile([P, ROW_TILES], F32)
@@ -198,24 +209,28 @@ def tile_deter_pb_t_kernel(tc, hid0, deter, hw1, hb1, hg1, gw, gb, out):
             def normalise(i):
                 c, j = divmod(i, ROW_TILES)
                 normed = work.tile([P, WIDTH], F32)
-                nc.vector.tensor_scalar_mul(
-                    out=normed[:], in0=gained[i][:], scalar1=inv_rms_of[c][:, j : j + 1]
+                nc.vector.scalar_tensor_tensor(
+                    out=normed[:], in0=biased[i][:], scalar=inv_rms_of[c][:, j : j + 1],
+                    in1=hg_all[:], op0=ALU.mult, op1=ALU.mult,
                 )
-                return normed
+                normed_of[i] = normed
 
-            def transpose_and_silu(i, normed):
+            def transpose_normed(i):
+                normed_t = psum.tile([P, COL_TILES, P], F32)
+                for t in range(COL_TILES):
+                    nc.tensor.transpose(
+                        normed_t[:, t, :], normed_of[i][:, t * P : (t + 1) * P], ident_f32[:]
+                    )
+                normed_t_of[i] = normed_t
+
+            def silu(i):
                 c, j = divmod(i, ROW_TILES)
                 if j == 0:
                     h_grouped = stage.tile([P, ROW_TILES, P, PACK], BF16, align_bytes=64)
                     h_grouped_of[c] = h_grouped
-                normed_t = psum.tile([P, COL_TILES, P], F32)
-                for t in range(COL_TILES):
-                    nc.tensor.transpose(
-                        normed_t[:, t, :], normed[:, t * P : (t + 1) * P], ident_f32[:]
-                    )
                 nc.scalar.activation(
                     out=h_grouped_of[c][:, j, :, :],
-                    in_=normed_t[:].rearrange("p t b -> p b t"),
+                    in_=normed_t_of[i][:].rearrange("p t b -> p b t"),
                     func=ACT.Silu,
                 )
 
@@ -230,35 +245,45 @@ def tile_deter_pb_t_kernel(tc, hid0, deter, hw1, hb1, hg1, gw, gb, out):
             transpose_x(0)
             copy_x(0)
             quantise_x(0)
-            for i in range(N_ROW_TILES + LAG + 1):
+            for i in range(N_ROW_TILES + NORM_LAG + 4):
                 c, j = divmod(i, ROW_TILES)
-                late = i - LAG
-                if 0 <= late < N_ROW_TILES:
-                    normed = normalise(late)
-                if i < N_ROW_TILES:
-                    if j == 0 and c + 1 < N_CHUNKS:
-                        transpose_x(c + 1)
-                    u_sb = product(i)
-                if 0 <= late < N_ROW_TILES:
-                    transpose_and_silu(late, normed)
-                if i < N_ROW_TILES:
-                    if j == 1 and c + 1 < N_CHUNKS:
-                        copy_x(c + 1)
-                    squares_and_gain(i, u_sb)
-                    if j == ROW_TILES - 1 and c + 1 < N_CHUNKS:
-                        quantise_x(c + 1)
-                if j == 0 and 1 <= c <= N_CHUNKS:
-                    inverse_rms(c - 1)
-                if late >= ROW_TILES and late % ROW_TILES == 0:
-                    quantise_h(late // ROW_TILES - 1)
-                if i < LAG and i % (LAG // GATES) == 1:
-                    quantise_weight(nc, stage, gw_raw, gw_codes, gw_scales, i // (LAG // GATES))
+                if is_row_tile(i - 1):
+                    add_bias(i - 1)
+                if is_row_tile(i):
+                    product(i)
+                if is_row_tile(i - 2):
+                    sum_squares(i - 2)
+                if is_row_tile(i - NORM_LAG):
+                    normalise(i - NORM_LAG)
+                if is_row_tile(i - NORM_LAG - 1):
+                    transpose_normed(i - NORM_LAG - 1)
+                if is_row_tile(i - NORM_LAG - 2):
+                    silu(i - NORM_LAG - 2)
+                if j == 0 and is_chunk(c + 1):
+                    transpose_x(c + 1)
+                if j == 1 and is_chunk(c + 1):
+                    copy_x(c + 1)
+                if j == 3 and is_chunk(c + 1):
+                    quantise_x(c + 1)
+                if (i - 2) % ROW_TILES == 3 and is_chunk((i - 2) // ROW_TILES):
+                    inverse_rms((i - 2) // ROW_TILES)
+                if (i - NORM_LAG - 3) % ROW_TILES == 3 and is_chunk((i - NORM_LAG - 3) // ROW_TILES):
+                    quantise_h((i - NORM_LAG - 3) // ROW_TILES)
+                if i < 2 * GATES and i % 2 == 1:
+                    quantise_weight(nc, stage, gw_raw, gw_codes, gw_scales, i // 2)
 
         with tc.psum_pool(name="psum_two", bufs=1, reuse_waits="tile") as psum:
             gate_banks = {}
             deter_t = {}
-            resets, updates, cands, steps, moves = {}, {}, {}, {}, {}
-            out_rows_of = {}
+            move_t_of = {}
+            resets, updates, gateds, cands, steps, moves = {}, {}, {}, {}, {}, {}
+
+            def is_unit(n):
+                return 0 <= n < N_UNITS
+
+            def bias_of(g, n):
+                col = g * COL_TILES + n % COL_TILES
+                return gate_bias[:, col : col + 1]
 
             def gate_products(n):
                 c, t = divmod(n, COL_TILES)
@@ -266,7 +291,7 @@ def tile_deter_pb_t_kernel(tc, hid0, deter, hw1, hb1, hg1, gw, gb, out):
                 gate_banks[n] = []
                 for g in range(GATES):
                     g_cols = slice(g * WIDTH + t * P, g * WIDTH + (t + 1) * P)
-                    g_ps = psum.tile([P, CHUNK], F32, bufs=2 * GATES)
+                    g_ps = psum.tile([P, CHUNK], F32, bufs=5)
                     nc.tensor.matmul_mx(
                         out=g_ps[:],
                         lhsT=gw_codes[:, g_cols].bitcast(FP8X4),
@@ -280,37 +305,38 @@ def tile_deter_pb_t_kernel(tc, hid0, deter, hw1, hb1, hg1, gw, gb, out):
 
             def transpose_deter(n):
                 c, t = divmod(n, COL_TILES)
-                d_t = psum.tile([P, ROW_TILES, P], BF16)
+                d_t = psum.tile([P, ROW_TILES, P], BF16, bufs=2)
                 for j in range(ROW_TILES):
                     nc.tensor.transpose(
                         d_t[:, j, :], d_chunks[c][:, j, t * P : (t + 1) * P], ident_bf16[:]
                     )
                 deter_t[n] = d_t
 
-            def bias_of(g, n):
-                col = g * COL_TILES + n % COL_TILES
-                return gate_bias[:, col : col + 1]
-
-            def reset_and_update(n):
+            def reset_gate(n):
                 reset = work.tile([P, CHUNK], F32)
                 nc.scalar.activation(
                     out=reset[:], in_=gate_banks[n][0][:], func=ACT.Sigmoid, bias=bias_of(0, n)
                 )
                 resets[n] = reset
-                update = work.tile([P, CHUNK], F32)
+
+            def update_gate(n):
+                update = work.tile([P, CHUNK], F32, bufs=4)
                 nc.scalar.activation(
                     out=update[:], in_=gate_banks[n][2][:], func=ACT.Sigmoid, bias=bias_of(2, n)
                 )
                 updates[n] = update
 
-            def candidate(n):
+            def gate_candidate(n):
                 gated = work.tile([P, CHUNK], F32)
                 nc.vector.scalar_tensor_tensor(
                     out=gated[:], in0=gate_banks[n][1][:], scalar=bias_of(1, n), in1=resets[n][:],
                     op0=ALU.add, op1=ALU.mult,
                 )
+                gateds[n] = gated
+
+            def candidate(n):
                 cand = work.tile([P, CHUNK], F32)
-                nc.scalar.activation(out=cand[:], in_=gated[:], func=ACT.Tanh)
+                nc.scalar.activation(out=cand[:], in_=gateds[n][:], func=ACT.Tanh)
                 cands[n] = cand
 
             def step_towards_candidate(n):
@@ -322,7 +348,7 @@ def tile_deter_pb_t_kernel(tc, hid0, deter, hw1, hb1, hg1, gw, gb, out):
                 steps[n] = step
 
             def scale_step(n):
-                move = work.tile([P, CHUNK], F32)
+                move = work.tile([P, CHUNK], F32, bufs=4)
                 nc.gpsimd.tensor_tensor(out=move[:], in0=steps[n][:], in1=updates[n][:], op=ALU.mult)
                 moves[n] = move
 
@@ -332,34 +358,35 @@ def tile_deter_pb_t_kernel(tc, hid0, deter, hw1, hb1, hg1, gw, gb, out):
                     nc.tensor.transpose(
                         move_t[:, j, :], moves[n][:, j * P : (j + 1) * P], ident_f32[:]
                     )
-                return move_t
+                move_t_of[n] = move_t
 
-            def finish(n, move_t):
+            def finish(n):
                 c, t = divmod(n, COL_TILES)
                 feats = slice(t * P, (t + 1) * P)
-                if t == 0:
-                    out_rows = work.tile([P, ROW_TILES, WIDTH], F32, bufs=2)
-                    out_rows_of[c] = out_rows
+                out_cols = work.tile([P, ROW_TILES, P], F32, bufs=4)
                 nc.vector.tensor_tensor(
-                    out=out_rows_of[c][:, :, feats], in0=move_t[:], in1=d_chunks[c][:, :, feats],
-                    op=ALU.add,
+                    out=out_cols[:], in0=move_t_of[n][:], in1=d_chunks[c][:, :, feats], op=ALU.add
                 )
-                if t == COL_TILES - 1:
-                    nc.sync.dma_start(out=chunk_view(out, c), in_=out_rows_of[c][:])
+                nc.sync.dma_start(out=chunk_view(out, c)[:, :, feats], in_=out_cols[:])
 
             gate_products(0)
-            for n in range(N_UNITS + 2):
-                if 1 <= n <= N_UNITS:
-                    step_towards_candidate(n - 1)
-                if n >= 2:
-                    move_t = transpose_move(n - 2)
-                if n + 1 < N_UNITS:
+            for n in range(N_UNITS + 5):
+                if is_unit(n - 2):
+                    step_towards_candidate(n - 2)
+                if is_unit(n - 4):
+                    transpose_move(n - 4)
+                if is_unit(n - 1):
+                    transpose_deter(n - 1)
+                if is_unit(n):
+                    reset_gate(n)
+                if is_unit(n - 1):
+                    candidate(n - 1)
+                if is_unit(n - 4):
+                    finish(n - 4)
+                if is_unit(n):
+                    gate_candidate(n)
+                    update_gate(n)
+                if is_unit(n + 1):
                     gate_products(n + 1)
-                if n < N_UNITS:
-                    transpose_deter(n)
-                    reset_and_update(n)
-                    candidate(n)
-                if 1 <= n <= N_UNITS:
-                    scale_step(n - 1)
-                if n >= 2:
-                    finish(n - 2, move_t)
+                if is_unit(n - 2):
+                    scale_step(n - 2)

@@ -14,6 +14,9 @@ PACK = 4
 BATCH = 4096
 WIDTH = 512
 GATES = 3
+R = 0
+C = 1
+Z = 2
 EPS = 1e-4
 CHUNK = 512
 ROW_TILES = CHUNK // P
@@ -21,7 +24,12 @@ COL_TILES = WIDTH // P
 N_CHUNKS = BATCH // CHUNK
 N_ROW_TILES = BATCH // P
 N_UNITS = N_CHUNKS * COL_TILES
-NORM_LAG = 8
+BIAS_LAG = 1
+SQUARE_LAG = 3
+NORM_LAG = 10
+TRANSPOSE_LAG = 11
+SILU_LAG = 13
+PACK_LAG = 14
 QUANT_COLS = 512
 
 FLOPS = 2 * BATCH * WIDTH * (WIDTH + GATES * WIDTH)
@@ -52,21 +60,24 @@ def tile_deter_pb_t_kernel(tc, hid0, deter, hw1, hb1, hg1, gw, gb, out):
     with tc.tile_pool(name="const", bufs=1) as const, tc.tile_pool(
         name="stage", bufs=2
     ) as stage, tc.tile_pool(name="work", bufs=3) as work, tc.manual_schedule():
+        x_chunks = []
+        for c in range(N_CHUNKS):
+            x_rows = const.tile([P, ROW_TILES, WIDTH], BF16, name="x_rows%d" % c)
+            x_chunks.append(x_rows)
+        nc.sync.dma_start(out=x_chunks[0][:], in_=chunk_view(hid0, 0))
         hw_raw = const.tile([P, PACK, WIDTH], BF16)
         for u in range(2):
             nc.sync.dma_start(
                 out=hw_raw[:, 2 * u : 2 * u + 2, :],
                 in_=hw1_rows[256 * u : 256 * (u + 1), :].rearrange("(q e) c -> q e c", e=2),
             )
-        x_chunks = []
-        for c in range(N_CHUNKS):
-            x_rows = const.tile([P, ROW_TILES, WIDTH], BF16, name="x_rows%d" % c)
-            x_chunks.append(x_rows)
-        nc.sync.dma_start(out=x_chunks[0][:], in_=chunk_view(hid0, 0))
-        nc.sync.dma_start(out=x_chunks[1][:], in_=chunk_view(hid0, 1))
         gw_raw = const.tile([P, PACK, GATES * WIDTH], BF16)
-        nc.sync.dma_start(out=gw_raw[:], in_=gw_rows.rearrange("(t p) n -> p t n", p=P))
-        for c in range(2, N_CHUNKS):
+        for g in range(GATES):
+            g_cols = slice(g * WIDTH, (g + 1) * WIDTH)
+            nc.sync.dma_start(
+                out=gw_raw[:, :, g_cols], in_=gw_rows[:, g_cols].rearrange("(t p) n -> p t n", p=P)
+            )
+        for c in range(1, N_CHUNKS):
             nc.sync.dma_start(out=x_chunks[c][:], in_=chunk_view(hid0, c))
         d_chunks = []
         for c in range(N_CHUNKS):
@@ -95,7 +106,6 @@ def tile_deter_pb_t_kernel(tc, hid0, deter, hw1, hb1, hg1, gw, gb, out):
 
         hw_codes = const.tile([P, WIDTH], U32, align_bytes=64)
         hw_scales = const.tile([P, WIDTH], U8, align_bytes=64)
-        quantise_weight(nc, stage, hw_raw, hw_codes, hw_scales, 0)
         gw_codes = const.tile([P, GATES * WIDTH], U32, align_bytes=64)
         gw_scales = const.tile([P, GATES * WIDTH], U8, align_bytes=64)
 
@@ -177,7 +187,7 @@ def tile_deter_pb_t_kernel(tc, hid0, deter, hw1, hb1, hg1, gw, gb, out):
                 products[i] = u_ps
 
             def add_bias(i):
-                u_sb = work.tile([P, WIDTH], F32, bufs=NORM_LAG + 1)
+                u_sb = work.tile([P, WIDTH], F32, bufs=NORM_LAG - BIAS_LAG + 2)
                 nc.vector.tensor_tensor(
                     out=u_sb[:], in0=products[i][:], in1=hb_all[:], op=ALU.add
                 )
@@ -242,37 +252,42 @@ def tile_deter_pb_t_kernel(tc, hid0, deter, hw1, hb1, hg1, gw, gb, out):
                     in_=h_grouped_of[c][:].rearrange("p j b t -> p (j b t)"),
                 )
 
+            def last_of_chunk(i):
+                return i // ROW_TILES if i % ROW_TILES == ROW_TILES - 1 else -1
+
             transpose_x(0)
+            quantise_weight(nc, stage, hw_raw, hw_codes, hw_scales, 0)
             copy_x(0)
             quantise_x(0)
-            for i in range(N_ROW_TILES + NORM_LAG + 4):
+            quantise_weight(nc, stage, gw_raw, gw_codes, gw_scales, 0)
+            for i in range(N_ROW_TILES + PACK_LAG + 1):
                 c, j = divmod(i, ROW_TILES)
-                if is_row_tile(i - 1):
-                    add_bias(i - 1)
-                if is_row_tile(i):
-                    product(i)
-                if is_row_tile(i - 2):
-                    sum_squares(i - 2)
                 if is_row_tile(i - NORM_LAG):
                     normalise(i - NORM_LAG)
-                if is_row_tile(i - NORM_LAG - 1):
-                    transpose_normed(i - NORM_LAG - 1)
-                if is_row_tile(i - NORM_LAG - 2):
-                    silu(i - NORM_LAG - 2)
-                if j == 0 and is_chunk(c + 1):
-                    transpose_x(c + 1)
-                if j == 1 and is_chunk(c + 1):
-                    copy_x(c + 1)
+                if is_row_tile(i - BIAS_LAG):
+                    add_bias(i - BIAS_LAG)
                 if j == 3 and is_chunk(c + 1):
                     quantise_x(c + 1)
-                if (i - 2) % ROW_TILES == 3 and is_chunk((i - 2) // ROW_TILES):
-                    inverse_rms((i - 2) // ROW_TILES)
-                if (i - NORM_LAG - 3) % ROW_TILES == 3 and is_chunk((i - NORM_LAG - 3) // ROW_TILES):
-                    quantise_h((i - NORM_LAG - 3) // ROW_TILES)
-                if i < 2 * GATES and i % 2 == 1:
-                    quantise_weight(nc, stage, gw_raw, gw_codes, gw_scales, i // 2)
+                if is_chunk(last_of_chunk(i - PACK_LAG)):
+                    quantise_h(last_of_chunk(i - PACK_LAG))
+                if i % 2 == 1 and 1 + i // 2 < GATES:
+                    quantise_weight(nc, stage, gw_raw, gw_codes, gw_scales, 1 + i // 2)
+                if is_row_tile(i - TRANSPOSE_LAG):
+                    transpose_normed(i - TRANSPOSE_LAG)
+                if is_row_tile(i):
+                    product(i)
+                if j == 0 and is_chunk(c + 1):
+                    transpose_x(c + 1)
+                if is_row_tile(i - SILU_LAG):
+                    silu(i - SILU_LAG)
+                if is_row_tile(i - SQUARE_LAG):
+                    sum_squares(i - SQUARE_LAG)
+                if j == 1 and is_chunk(c + 1):
+                    copy_x(c + 1)
+                if is_chunk(last_of_chunk(i - SQUARE_LAG)):
+                    inverse_rms(last_of_chunk(i - SQUARE_LAG))
 
-        with tc.psum_pool(name="psum_two", bufs=1, reuse_waits="tile") as psum:
+        with tc.psum_pool(name="psum_two", bufs=8, reuse_waits="tile") as psum:
             gate_banks = {}
             deter_t = {}
             move_t_of = {}
@@ -285,27 +300,25 @@ def tile_deter_pb_t_kernel(tc, hid0, deter, hw1, hb1, hg1, gw, gb, out):
                 col = g * COL_TILES + n % COL_TILES
                 return gate_bias[:, col : col + 1]
 
-            def gate_products(n):
+            def gate_product(g, n):
                 c, t = divmod(n, COL_TILES)
                 cols = slice(c * CHUNK, (c + 1) * CHUNK)
-                gate_banks[n] = []
-                for g in range(GATES):
-                    g_cols = slice(g * WIDTH + t * P, g * WIDTH + (t + 1) * P)
-                    g_ps = psum.tile([P, CHUNK], F32, bufs=5)
-                    nc.tensor.matmul_mx(
-                        out=g_ps[:],
-                        lhsT=gw_codes[:, g_cols].bitcast(FP8X4),
-                        lhsT_scale=gw_scales[:, g_cols],
-                        rhs=h_codes[:, cols].bitcast(FP8X4),
-                        rhs_scale=h_scales[:, cols],
-                        start=True,
-                        stop=True,
-                    )
-                    gate_banks[n].append(g_ps)
+                g_cols = slice(g * WIDTH + t * P, g * WIDTH + (t + 1) * P)
+                g_ps = psum.tile([P, CHUNK], F32, tag="bank")
+                nc.tensor.matmul_mx(
+                    out=g_ps[:],
+                    lhsT=gw_codes[:, g_cols].bitcast(FP8X4),
+                    lhsT_scale=gw_scales[:, g_cols],
+                    rhs=h_codes[:, cols].bitcast(FP8X4),
+                    rhs_scale=h_scales[:, cols],
+                    start=True,
+                    stop=True,
+                )
+                gate_banks[(g, n)] = g_ps
 
             def transpose_deter(n):
                 c, t = divmod(n, COL_TILES)
-                d_t = psum.tile([P, ROW_TILES, P], BF16, bufs=2)
+                d_t = psum.tile([P, ROW_TILES, P], BF16, tag="bank")
                 for j in range(ROW_TILES):
                     nc.tensor.transpose(
                         d_t[:, j, :], d_chunks[c][:, j, t * P : (t + 1) * P], ident_bf16[:]
@@ -315,21 +328,21 @@ def tile_deter_pb_t_kernel(tc, hid0, deter, hw1, hb1, hg1, gw, gb, out):
             def reset_gate(n):
                 reset = work.tile([P, CHUNK], F32)
                 nc.scalar.activation(
-                    out=reset[:], in_=gate_banks[n][0][:], func=ACT.Sigmoid, bias=bias_of(0, n)
+                    out=reset[:], in_=gate_banks[(R, n)][:], func=ACT.Sigmoid, bias=bias_of(R, n)
                 )
                 resets[n] = reset
 
             def update_gate(n):
                 update = work.tile([P, CHUNK], F32, bufs=4)
                 nc.scalar.activation(
-                    out=update[:], in_=gate_banks[n][2][:], func=ACT.Sigmoid, bias=bias_of(2, n)
+                    out=update[:], in_=gate_banks[(Z, n)][:], func=ACT.Sigmoid, bias=bias_of(Z, n)
                 )
                 updates[n] = update
 
             def gate_candidate(n):
                 gated = work.tile([P, CHUNK], F32)
                 nc.vector.scalar_tensor_tensor(
-                    out=gated[:], in0=gate_banks[n][1][:], scalar=bias_of(1, n), in1=resets[n][:],
+                    out=gated[:], in0=gate_banks[(C, n)][:], scalar=bias_of(C, n), in1=resets[n][:],
                     op0=ALU.add, op1=ALU.mult,
                 )
                 gateds[n] = gated
@@ -353,7 +366,7 @@ def tile_deter_pb_t_kernel(tc, hid0, deter, hw1, hb1, hg1, gw, gb, out):
                 moves[n] = move
 
             def transpose_move(n):
-                move_t = psum.tile([P, ROW_TILES, P], F32)
+                move_t = psum.tile([P, ROW_TILES, P], F32, tag="bank")
                 for j in range(ROW_TILES):
                     nc.tensor.transpose(
                         move_t[:, j, :], moves[n][:, j * P : (j + 1) * P], ident_f32[:]
@@ -369,24 +382,26 @@ def tile_deter_pb_t_kernel(tc, hid0, deter, hw1, hb1, hg1, gw, gb, out):
                 )
                 nc.sync.dma_start(out=chunk_view(out, c)[:, :, feats], in_=out_cols[:])
 
-            gate_products(0)
-            for n in range(N_UNITS + 5):
-                if is_unit(n - 2):
-                    step_towards_candidate(n - 2)
+            for n in range(-1, N_UNITS + 5):
+                if is_unit(n + 1):
+                    gate_product(R, n + 1)
+                    gate_product(Z, n + 1)
                 if is_unit(n - 4):
                     transpose_move(n - 4)
-                if is_unit(n - 1):
-                    transpose_deter(n - 1)
                 if is_unit(n):
                     reset_gate(n)
+                    update_gate(n)
                 if is_unit(n - 1):
                     candidate(n - 1)
-                if is_unit(n - 4):
-                    finish(n - 4)
+                if is_unit(n - 1):
+                    transpose_deter(n - 1)
+                if is_unit(n + 1):
+                    gate_product(C, n + 1)
+                if is_unit(n - 2):
+                    step_towards_candidate(n - 2)
                 if is_unit(n):
                     gate_candidate(n)
-                    update_gate(n)
-                if is_unit(n + 1):
-                    gate_products(n + 1)
+                if is_unit(n - 4):
+                    finish(n - 4)
                 if is_unit(n - 2):
                     scale_step(n - 2)

@@ -29,6 +29,7 @@ SQUARE_LAG = 3
 NORM_LAG = 10
 TRANSPOSE_LAG = 11
 SILU_LAG = 13
+PASSES_PER_PRODUCT = 2
 PACK_LAG = 14
 QUANT_COLS = 512
 
@@ -175,15 +176,16 @@ def tile_deter_pb_t_kernel(tc, hid0, deter, hw1, hb1, hg1, gw, gb, out):
                 x_codes, x_scales = x_packed[c]
                 rows = slice(j * P, (j + 1) * P)
                 u_ps = psum.tile([P, WIDTH], F32)
-                nc.tensor.matmul_mx(
-                    out=u_ps[:],
-                    lhsT=x_codes[:, rows].bitcast(FP8X4),
-                    lhsT_scale=x_scales[:, rows],
-                    rhs=hw_codes[:].bitcast(FP8X4),
-                    rhs_scale=hw_scales[:],
-                    start=True,
-                    stop=True,
-                )
+                for repeat in range(PASSES_PER_PRODUCT):
+                    nc.tensor.matmul_mx(
+                        out=u_ps[:],
+                        lhsT=x_codes[:, rows].bitcast(FP8X4),
+                        lhsT_scale=x_scales[:, rows],
+                        rhs=hw_codes[:].bitcast(FP8X4),
+                        rhs_scale=hw_scales[:],
+                        start=True,
+                        stop=True,
+                    )
                 products[i] = u_ps
 
             def add_bias(i):

@@ -25,12 +25,13 @@ N_CHUNKS = BATCH // CHUNK
 N_ROW_TILES = BATCH // P
 N_UNITS = N_CHUNKS * COL_TILES
 BIAS_LAG = 1
-SQUARE_LAG = 3
-NORM_LAG = 10
-TRANSPOSE_LAG = 11
-SILU_LAG = 13
-PASSES_PER_PRODUCT = 2
-PACK_LAG = 14
+SQUARE_LAG = 4
+RMS_LAG = 6
+NORM_LAG = 11
+TRANSPOSE_LAG = 12
+SILU_LAG = 14
+PACK_LAG = 15
+DETER_BUFS = 4
 QUANT_COLS = 512
 
 FLOPS = 2 * BATCH * WIDTH * (WIDTH + GATES * WIDTH)
@@ -80,11 +81,15 @@ def tile_deter_pb_t_kernel(tc, hid0, deter, hw1, hb1, hg1, gw, gb, out):
             )
         for c in range(1, N_CHUNKS):
             nc.sync.dma_start(out=x_chunks[c][:], in_=chunk_view(hid0, c))
-        d_chunks = []
-        for c in range(N_CHUNKS):
-            d_rows = const.tile([P, ROW_TILES, WIDTH], BF16, name="d_rows%d" % c)
+        d_chunks = {}
+
+        def load_deter(c):
+            d_rows = work.tile([P, ROW_TILES, WIDTH], BF16, bufs=DETER_BUFS)
             nc.sync.dma_start(out=d_rows[:], in_=chunk_view(deter, c))
-            d_chunks.append(d_rows)
+            d_chunks[c] = d_rows
+
+        for c in range(DETER_BUFS):
+            load_deter(c)
 
         gb_rows = const.tile([P, P], BF16)
         nc.vector.memset(gb_rows[:], 0.0)
@@ -176,20 +181,19 @@ def tile_deter_pb_t_kernel(tc, hid0, deter, hw1, hb1, hg1, gw, gb, out):
                 x_codes, x_scales = x_packed[c]
                 rows = slice(j * P, (j + 1) * P)
                 u_ps = psum.tile([P, WIDTH], F32)
-                for repeat in range(PASSES_PER_PRODUCT):
-                    nc.tensor.matmul_mx(
-                        out=u_ps[:],
-                        lhsT=x_codes[:, rows].bitcast(FP8X4),
-                        lhsT_scale=x_scales[:, rows],
-                        rhs=hw_codes[:].bitcast(FP8X4),
-                        rhs_scale=hw_scales[:],
-                        start=True,
-                        stop=True,
-                    )
+                nc.tensor.matmul_mx(
+                    out=u_ps[:],
+                    lhsT=x_codes[:, rows].bitcast(FP8X4),
+                    lhsT_scale=x_scales[:, rows],
+                    rhs=hw_codes[:].bitcast(FP8X4),
+                    rhs_scale=hw_scales[:],
+                    start=True,
+                    stop=True,
+                )
                 products[i] = u_ps
 
             def add_bias(i):
-                u_sb = work.tile([P, WIDTH], F32, bufs=NORM_LAG - BIAS_LAG + 2)
+                u_sb = work.tile([P, WIDTH], F32, bufs=NORM_LAG - BIAS_LAG + 3)
                 nc.vector.tensor_tensor(
                     out=u_sb[:], in0=products[i][:], in1=hb_all[:], op=ALU.add
                 )
@@ -264,36 +268,37 @@ def tile_deter_pb_t_kernel(tc, hid0, deter, hw1, hb1, hg1, gw, gb, out):
             quantise_weight(nc, stage, gw_raw, gw_codes, gw_scales, 0)
             for i in range(N_ROW_TILES + PACK_LAG + 1):
                 c, j = divmod(i, ROW_TILES)
-                if is_row_tile(i - NORM_LAG):
-                    normalise(i - NORM_LAG)
-                if is_row_tile(i - BIAS_LAG):
-                    add_bias(i - BIAS_LAG)
-                if j == 3 and is_chunk(c + 1):
-                    quantise_x(c + 1)
-                if is_chunk(last_of_chunk(i - PACK_LAG)):
-                    quantise_h(last_of_chunk(i - PACK_LAG))
                 if i % 2 == 1 and 1 + i // 2 < GATES:
                     quantise_weight(nc, stage, gw_raw, gw_codes, gw_scales, 1 + i // 2)
-                if is_row_tile(i - TRANSPOSE_LAG):
-                    transpose_normed(i - TRANSPOSE_LAG)
-                if is_row_tile(i):
-                    product(i)
+                if is_row_tile(i - BIAS_LAG):
+                    add_bias(i - BIAS_LAG)
+                if is_row_tile(i - NORM_LAG):
+                    normalise(i - NORM_LAG)
+                if is_chunk(last_of_chunk(i - PACK_LAG)):
+                    quantise_h(last_of_chunk(i - PACK_LAG))
+                if j == 2 and is_chunk(c + 1):
+                    quantise_x(c + 1)
                 if j == 0 and is_chunk(c + 1):
                     transpose_x(c + 1)
+                if is_row_tile(i):
+                    product(i)
+                if is_row_tile(i - TRANSPOSE_LAG):
+                    transpose_normed(i - TRANSPOSE_LAG)
                 if is_row_tile(i - SILU_LAG):
                     silu(i - SILU_LAG)
                 if is_row_tile(i - SQUARE_LAG):
                     sum_squares(i - SQUARE_LAG)
                 if j == 1 and is_chunk(c + 1):
                     copy_x(c + 1)
-                if is_chunk(last_of_chunk(i - SQUARE_LAG)):
-                    inverse_rms(last_of_chunk(i - SQUARE_LAG))
+                if is_chunk(last_of_chunk(i - RMS_LAG)):
+                    inverse_rms(last_of_chunk(i - RMS_LAG))
 
-        with tc.psum_pool(name="psum_two", bufs=8, reuse_waits="tile") as psum:
+        with tc.psum_pool(name="psum_two", bufs=5, reuse_waits="tile") as psum:
             gate_banks = {}
             deter_t = {}
             move_t_of = {}
             resets, updates, gateds, cands, steps, moves = {}, {}, {}, {}, {}, {}
+            out_rows_of = {}
 
             def is_unit(n):
                 return 0 <= n < N_UNITS
@@ -306,7 +311,7 @@ def tile_deter_pb_t_kernel(tc, hid0, deter, hw1, hb1, hg1, gw, gb, out):
                 c, t = divmod(n, COL_TILES)
                 cols = slice(c * CHUNK, (c + 1) * CHUNK)
                 g_cols = slice(g * WIDTH + t * P, g * WIDTH + (t + 1) * P)
-                g_ps = psum.tile([P, CHUNK], F32, tag="bank")
+                g_ps = psum.tile([P, CHUNK], F32)
                 nc.tensor.matmul_mx(
                     out=g_ps[:],
                     lhsT=gw_codes[:, g_cols].bitcast(FP8X4),
@@ -320,7 +325,7 @@ def tile_deter_pb_t_kernel(tc, hid0, deter, hw1, hb1, hg1, gw, gb, out):
 
             def transpose_deter(n):
                 c, t = divmod(n, COL_TILES)
-                d_t = psum.tile([P, ROW_TILES, P], BF16, tag="bank")
+                d_t = psum.tile([P, ROW_TILES, P], BF16, tag="turned", bufs=3)
                 for j in range(ROW_TILES):
                     nc.tensor.transpose(
                         d_t[:, j, :], d_chunks[c][:, j, t * P : (t + 1) * P], ident_bf16[:]
@@ -335,7 +340,7 @@ def tile_deter_pb_t_kernel(tc, hid0, deter, hw1, hb1, hg1, gw, gb, out):
                 resets[n] = reset
 
             def update_gate(n):
-                update = work.tile([P, CHUNK], F32, bufs=4)
+                update = work.tile([P, CHUNK], F32, bufs=5)
                 nc.scalar.activation(
                     out=update[:], in_=gate_banks[(Z, n)][:], func=ACT.Sigmoid, bias=bias_of(Z, n)
                 )
@@ -363,12 +368,12 @@ def tile_deter_pb_t_kernel(tc, hid0, deter, hw1, hb1, hg1, gw, gb, out):
                 steps[n] = step
 
             def scale_step(n):
-                move = work.tile([P, CHUNK], F32, bufs=4)
+                move = work.tile([P, CHUNK], F32, bufs=5)
                 nc.gpsimd.tensor_tensor(out=move[:], in0=steps[n][:], in1=updates[n][:], op=ALU.mult)
                 moves[n] = move
 
             def transpose_move(n):
-                move_t = psum.tile([P, ROW_TILES, P], F32, tag="bank")
+                move_t = psum.tile([P, ROW_TILES, P], F32, tag="turned", bufs=3)
                 for j in range(ROW_TILES):
                     nc.tensor.transpose(
                         move_t[:, j, :], moves[n][:, j * P : (j + 1) * P], ident_f32[:]
@@ -378,32 +383,41 @@ def tile_deter_pb_t_kernel(tc, hid0, deter, hw1, hb1, hg1, gw, gb, out):
             def finish(n):
                 c, t = divmod(n, COL_TILES)
                 feats = slice(t * P, (t + 1) * P)
-                out_cols = work.tile([P, ROW_TILES, P], F32, bufs=4)
+                if t == 0:
+                    out_rows = work.tile([P, ROW_TILES, WIDTH], F32, bufs=2)
+                    out_rows_of[c] = out_rows
                 nc.vector.tensor_tensor(
-                    out=out_cols[:], in0=move_t_of[n][:], in1=d_chunks[c][:, :, feats], op=ALU.add
+                    out=out_rows_of[c][:, :, feats], in0=move_t_of[n][:],
+                    in1=d_chunks[c][:, :, feats], op=ALU.add,
                 )
-                nc.sync.dma_start(out=chunk_view(out, c)[:, :, feats], in_=out_cols[:])
+                nc.sync.dma_start(
+                    out=chunk_view(out, c)[:, :, feats], in_=out_rows_of[c][:, :, feats]
+                )
 
             for n in range(-1, N_UNITS + 5):
-                if is_unit(n + 1):
-                    gate_product(R, n + 1)
-                    gate_product(Z, n + 1)
-                if is_unit(n - 4):
-                    transpose_move(n - 4)
+                ahead = n // COL_TILES + 2
+                if n % COL_TILES == 0 and DETER_BUFS <= ahead < N_CHUNKS:
+                    load_deter(ahead)
                 if is_unit(n):
                     reset_gate(n)
-                    update_gate(n)
                 if is_unit(n - 1):
                     candidate(n - 1)
+                if is_unit(n):
+                    update_gate(n)
+                if is_unit(n + 1):
+                    gate_product(R, n + 1)
+                    gate_product(C, n + 1)
+                if is_unit(n - 4):
+                    transpose_move(n - 4)
                 if is_unit(n - 1):
                     transpose_deter(n - 1)
                 if is_unit(n + 1):
-                    gate_product(C, n + 1)
-                if is_unit(n - 2):
-                    step_towards_candidate(n - 2)
+                    gate_product(Z, n + 1)
                 if is_unit(n):
                     gate_candidate(n)
+                if is_unit(n - 2):
+                    step_towards_candidate(n - 2)
                 if is_unit(n - 4):
                     finish(n - 4)
-                if is_unit(n - 2):
-                    scale_step(n - 2)
+                if is_unit(n - 3):
+                    scale_step(n - 3)

import concourse.mybir as mybir
from concourse.masks import make_identity

F32 = mybir.dt.float32
BF16 = mybir.dt.bfloat16
U32 = mybir.dt.uint32
U8 = mybir.dt.uint8
FP8X4 = mybir.dt.float8_e4m3fn_x4
ACT = mybir.ActivationFunctionType
ALU = mybir.AluOpType

P = 128
PACK = 4
BATCH = 4096
WIDTH = 512
GATES = 3
R = 0
C = 1
Z = 2
EPS = 1e-4
CHUNK = 512
ROW_TILES = CHUNK // P
COL_TILES = WIDTH // P
N_CHUNKS = BATCH // CHUNK
N_ROW_TILES = BATCH // P
N_UNITS = N_CHUNKS * COL_TILES
BIAS_LAG = 1
SQUARE_LAG = 4
RMS_LAG = 6
NORM_LAG = 11
TRANSPOSE_LAG = 12
SILU_LAG = 14
PACK_LAG = 15
DETER_BUFS = 4
QUANT_COLS = 512

FLOPS = 2 * BATCH * WIDTH * (WIDTH + GATES * WIDTH)


def quantise_weight(nc, stage, raw, codes, scales, piece):
    cols = slice(piece * QUANT_COLS, (piece + 1) * QUANT_COLS)
    grouped = stage.tile([P, QUANT_COLS, PACK], BF16, align_bytes=64)
    nc.vector.tensor_copy(
        out=grouped[:].rearrange("p (c i) t -> p c t i", i=4),
        in_=raw[:, :, cols].rearrange("p t (c i) -> p c t i", i=4),
    )
    nc.vector.quantize_mx(
        out=codes[:, cols].bitcast(FP8X4),
        scales=scales[:, cols],
        in_=grouped[:].rearrange("p c t -> p (c t)"),
    )


def tile_deter_pb_t_kernel(tc, hid0, deter, hw1, hb1, hg1, gw, gb, out):
    nc = tc.nc
    hw1_rows = hw1.rearrange("o k f -> (o k) f")
    gw_rows = gw.rearrange("o k n -> (o k) n")

    def chunk_view(dram, c):
        return dram[c * CHUNK : (c + 1) * CHUNK, :].rearrange("(p j) f -> p j f", j=ROW_TILES)

    with tc.tile_pool(name="const", bufs=1) as const, tc.tile_pool(
        name="stage", bufs=2
    ) as stage, tc.tile_pool(name="work", bufs=3) as work, tc.manual_schedule():
        x_chunks = []
        for c in range(N_CHUNKS):
            x_rows = const.tile([P, ROW_TILES, WIDTH], BF16, name="x_rows%d" % c)
            x_chunks.append(x_rows)
        nc.sync.dma_start(out=x_chunks[0][:], in_=chunk_view(hid0, 0))
        hw_raw = const.tile([P, PACK, WIDTH], BF16)
        for u in range(2):
            nc.sync.dma_start(
                out=hw_raw[:, 2 * u : 2 * u + 2, :],
                in_=hw1_rows[256 * u : 256 * (u + 1), :].rearrange("(q e) c -> q e c", e=2),
            )
        gw_raw = const.tile([P, PACK, GATES * WIDTH], BF16)
        for g in range(GATES):
            g_cols = slice(g * WIDTH, (g + 1) * WIDTH)
            nc.sync.dma_start(
                out=gw_raw[:, :, g_cols], in_=gw_rows[:, g_cols].rearrange("(t p) n -> p t n", p=P)
            )
        for c in range(1, N_CHUNKS):
            nc.sync.dma_start(out=x_chunks[c][:], in_=chunk_view(hid0, c))
        d_chunks = {}

        def load_deter(c):
            d_rows = work.tile([P, ROW_TILES, WIDTH], BF16, bufs=DETER_BUFS)
            nc.sync.dma_start(out=d_rows[:], in_=chunk_view(deter, c))
            d_chunks[c] = d_rows

        for c in range(DETER_BUFS):
            load_deter(c)

        gb_rows = const.tile([P, P], BF16)
        nc.vector.memset(gb_rows[:], 0.0)
        nc.scalar.dma_start(
            out=gb_rows[0 : GATES * COL_TILES, :], in_=gb.rearrange("(r c) -> r c", c=P)
        )
        hb_all = const.tile([P, WIDTH], BF16)
        hg_all = const.tile([P, WIDTH], BF16)
        nc.scalar.dma_start(out=hb_all[:], in_=hb1.partition_broadcast(P))
        nc.scalar.dma_start(out=hg_all[:], in_=hg1.partition_broadcast(P))

        minus_half = const.tile([P, ROW_TILES], F32)
        nc.vector.memset(minus_half[:], -0.5)
        warm = const.tile([P, 1], F32)
        nc.scalar.activation(out=warm[:], in_=minus_half[:, 0:1], func=ACT.Silu)
        ident_f32 = const.tile([P, P], F32)
        make_identity(nc, ident_f32[:])
        ident_bf16 = const.tile([P, P], BF16)
        make_identity(nc, ident_bf16[:])

        hw_codes = const.tile([P, WIDTH], U32, align_bytes=64)
        hw_scales = const.tile([P, WIDTH], U8, align_bytes=64)
        gw_codes = const.tile([P, GATES * WIDTH], U32, align_bytes=64)
        gw_scales = const.tile([P, GATES * WIDTH], U8, align_bytes=64)

        h_codes = const.tile([P, BATCH], U32, align_bytes=64)
        h_scales = const.tile([P, BATCH], U8, align_bytes=64)

        with tc.psum_pool(name="psum_one", bufs=3) as psum:
            gb_t = psum.tile([P, P], BF16, tag="x_t", bufs=2)
            nc.tensor.transpose(gb_t[:], gb_rows[:], ident_bf16[:])
            gate_bias = const.tile([P, GATES * COL_TILES], F32)
            nc.vector.tensor_copy(out=gate_bias[:], in_=gb_t[:, 0 : GATES * COL_TILES])
            z_bias = gate_bias[:, 2 * COL_TILES : 3 * COL_TILES]
            nc.vector.tensor_scalar_add(out=z_bias, in0=z_bias, scalar1=-1.0)

            x_banks = {}
            x_grouped_of = {}
            x_packed = {}
            products = {}
            biased = {}
            sum_sq_of = {}
            inv_rms_of = {}
            normed_of = {}
            normed_t_of = {}
            h_grouped_of = {}

            def is_chunk(c):
                return 0 <= c < N_CHUNKS

            def is_row_tile(i):
                return 0 <= i < N_ROW_TILES

            def transpose_x(c):
                x_banks[c] = []
                for pair in range(ROW_TILES // 2):
                    x_t = psum.tile([P, 2, 2, P], F32, tag="x_t", bufs=2)
                    for jj in range(2):
                        for u in range(2):
                            nc.tensor.transpose(
                                x_t[:, jj, u, :],
                                x_chunks[c][:, 2 * pair + jj, :].bitcast(F32)[:, u * P : (u + 1) * P],
                                ident_f32[:],
                            )
                    x_banks[c].append(x_t)

            def copy_x(c):
                x_grouped = stage.tile([P, CHUNK * PACK], BF16, align_bytes=64)
                x_words = x_grouped[:].bitcast(F32).rearrange(
                    "p (j b u) -> p j b u", j=ROW_TILES, u=2
                )
                for pair in range(ROW_TILES // 2):
                    nc.scalar.copy(
                        out=x_words[:, 2 * pair : 2 * pair + 2],
                        in_=x_banks[c][pair][:].rearrange("p j u b -> p j b u"),
                    )
                x_grouped_of[c] = x_grouped

            def quantise_x(c):
                x_codes = stage.tile([P, CHUNK], U32, align_bytes=64)
                x_scales = stage.tile([P, CHUNK], U8, align_bytes=64)
                nc.vector.quantize_mx(
                    out=x_codes[:].bitcast(FP8X4), scales=x_scales[:], in_=x_grouped_of[c][:]
                )
                x_packed[c] = (x_codes, x_scales)

            def product(i):
                c, j = divmod(i, ROW_TILES)
                x_codes, x_scales = x_packed[c]
                rows = slice(j * P, (j + 1) * P)
                u_ps = psum.tile([P, WIDTH], F32)
                nc.tensor.matmul_mx(
                    out=u_ps[:],
                    lhsT=x_codes[:, rows].bitcast(FP8X4),
                    lhsT_scale=x_scales[:, rows],
                    rhs=hw_codes[:].bitcast(FP8X4),
                    rhs_scale=hw_scales[:],
                    start=True,
                    stop=True,
                )
                products[i] = u_ps

            def add_bias(i):
                u_sb = work.tile([P, WIDTH], F32, bufs=NORM_LAG - BIAS_LAG + 3)
                nc.vector.tensor_tensor(
                    out=u_sb[:], in0=products[i][:], in1=hb_all[:], op=ALU.add
                )
                biased[i] = u_sb

            def sum_squares(i):
                c, j = divmod(i, ROW_TILES)
                if j == 0:
                    sum_sq = work.tile([P, ROW_TILES], F32)
                    sum_sq_of[c] = sum_sq
                squares = work.tile([P, WIDTH], BF16)
                nc.scalar.activation(
                    out=squares[:], in_=biased[i][:], func=ACT.Square,
                    accum_out=sum_sq_of[c][:, j : j + 1],
                )

            def inverse_rms(c):
                mean_sq = work.tile([P, ROW_TILES], F32)
                nc.gpsimd.tensor_scalar(
                    out=mean_sq[:], in0=sum_sq_of[c][:], scalar1=1.0 / WIDTH, scalar2=EPS,
                    op0=ALU.mult, op1=ALU.add,
                )
                inv_rms = work.tile([P, ROW_TILES], F32)
                nc.gpsimd.tensor_tensor(
                    out=inv_rms[:], in0=mean_sq[:], in1=minus_half[:], op=ALU.pow
                )
                inv_rms_of[c] = inv_rms

            def normalise(i):
                c, j = divmod(i, ROW_TILES)
                normed = work.tile([P, WIDTH], F32)
                nc.vector.scalar_tensor_tensor(
                    out=normed[:], in0=biased[i][:], scalar=inv_rms_of[c][:, j : j + 1],
                    in1=hg_all[:], op0=ALU.mult, op1=ALU.mult,
                )
                normed_of[i] = normed

            def transpose_normed(i):
                normed_t = psum.tile([P, COL_TILES, P], F32)
                for t in range(COL_TILES):
                    nc.tensor.transpose(
                        normed_t[:, t, :], normed_of[i][:, t * P : (t + 1) * P], ident_f32[:]
                    )
                normed_t_of[i] = normed_t

            def silu(i):
                c, j = divmod(i, ROW_TILES)
                if j == 0:
                    h_grouped = stage.tile([P, ROW_TILES, P, PACK], BF16, align_bytes=64)
                    h_grouped_of[c] = h_grouped
                nc.scalar.activation(
                    out=h_grouped_of[c][:, j, :, :],
                    in_=normed_t_of[i][:].rearrange("p t b -> p b t"),
                    func=ACT.Silu,
                )

            def quantise_h(c):
                cols = slice(c * CHUNK, (c + 1) * CHUNK)
                nc.vector.quantize_mx(
                    out=h_codes[:, cols].bitcast(FP8X4),
                    scales=h_scales[:, cols],
                    in_=h_grouped_of[c][:].rearrange("p j b t -> p (j b t)"),
                )

            def last_of_chunk(i):
                return i // ROW_TILES if i % ROW_TILES == ROW_TILES - 1 else -1

            transpose_x(0)
            quantise_weight(nc, stage, hw_raw, hw_codes, hw_scales, 0)
            copy_x(0)
            quantise_x(0)
            quantise_weight(nc, stage, gw_raw, gw_codes, gw_scales, 0)
            for i in range(N_ROW_TILES + PACK_LAG + 1):
                c, j = divmod(i, ROW_TILES)
                if i % 2 == 1 and 1 + i // 2 < GATES:
                    quantise_weight(nc, stage, gw_raw, gw_codes, gw_scales, 1 + i // 2)
                if is_row_tile(i - BIAS_LAG):
                    add_bias(i - BIAS_LAG)
                if is_row_tile(i - NORM_LAG):
                    normalise(i - NORM_LAG)
                if is_chunk(last_of_chunk(i - PACK_LAG)):
                    quantise_h(last_of_chunk(i - PACK_LAG))
                if j == 2 and is_chunk(c + 1):
                    quantise_x(c + 1)
                if j == 0 and is_chunk(c + 1):
                    transpose_x(c + 1)
                if is_row_tile(i):
                    product(i)
                if is_row_tile(i - TRANSPOSE_LAG):
                    transpose_normed(i - TRANSPOSE_LAG)
                if is_row_tile(i - SILU_LAG):
                    silu(i - SILU_LAG)
                if is_row_tile(i - SQUARE_LAG):
                    sum_squares(i - SQUARE_LAG)
                if j == 1 and is_chunk(c + 1):
                    copy_x(c + 1)
                if is_chunk(last_of_chunk(i - RMS_LAG)):
                    inverse_rms(last_of_chunk(i - RMS_LAG))

        with tc.psum_pool(name="psum_two", bufs=5, reuse_waits="tile") as psum:
            gate_banks = {}
            deter_t = {}
            move_t_of = {}
            resets, updates, gateds, cands, steps, moves = {}, {}, {}, {}, {}, {}
            out_rows_of = {}

            def is_unit(n):
                return 0 <= n < N_UNITS

            def bias_of(g, n):
                col = g * COL_TILES + n % COL_TILES
                return gate_bias[:, col : col + 1]

            def gate_product(g, n):
                c, t = divmod(n, COL_TILES)
                cols = slice(c * CHUNK, (c + 1) * CHUNK)
                g_cols = slice(g * WIDTH + t * P, g * WIDTH + (t + 1) * P)
                g_ps = psum.tile([P, CHUNK], F32)
                nc.tensor.matmul_mx(
                    out=g_ps[:],
                    lhsT=gw_codes[:, g_cols].bitcast(FP8X4),
                    lhsT_scale=gw_scales[:, g_cols],
                    rhs=h_codes[:, cols].bitcast(FP8X4),
                    rhs_scale=h_scales[:, cols],
                    start=True,
                    stop=True,
                )
                gate_banks[(g, n)] = g_ps

            def transpose_deter(n):
                c, t = divmod(n, COL_TILES)
                d_t = psum.tile([P, ROW_TILES, P], BF16, tag="turned", bufs=3)
                for j in range(ROW_TILES):
                    nc.tensor.transpose(
                        d_t[:, j, :], d_chunks[c][:, j, t * P : (t + 1) * P], ident_bf16[:]
                    )
                deter_t[n] = d_t

            def reset_gate(n):
                reset = work.tile([P, CHUNK], F32)
                nc.scalar.activation(
                    out=reset[:], in_=gate_banks[(R, n)][:], func=ACT.Sigmoid, bias=bias_of(R, n)
                )
                resets[n] = reset

            def update_gate(n):
                update = work.tile([P, CHUNK], F32, bufs=5)
                nc.scalar.activation(
                    out=update[:], in_=gate_banks[(Z, n)][:], func=ACT.Sigmoid, bias=bias_of(Z, n)
                )
                updates[n] = update

            def gate_candidate(n):
                gated = work.tile([P, CHUNK], F32)
                nc.vector.scalar_tensor_tensor(
                    out=gated[:], in0=gate_banks[(C, n)][:], scalar=bias_of(C, n), in1=resets[n][:],
                    op0=ALU.add, op1=ALU.mult,
                )
                gateds[n] = gated

            def candidate(n):
                cand = work.tile([P, CHUNK], F32)
                nc.scalar.activation(out=cand[:], in_=gateds[n][:], func=ACT.Tanh)
                cands[n] = cand

            def step_towards_candidate(n):
                step = work.tile([P, CHUNK], F32)
                nc.vector.tensor_tensor(
                    out=step[:], in0=cands[n][:], in1=deter_t[n][:].rearrange("p j b -> p (j b)"),
                    op=ALU.subtract,
                )
                steps[n] = step

            def scale_step(n):
                move = work.tile([P, CHUNK], F32, bufs=5)
                nc.gpsimd.tensor_tensor(out=move[:], in0=steps[n][:], in1=updates[n][:], op=ALU.mult)
                moves[n] = move

            def transpose_move(n):
                move_t = psum.tile([P, ROW_TILES, P], F32, tag="turned", bufs=3)
                for j in range(ROW_TILES):
                    nc.tensor.transpose(
                        move_t[:, j, :], moves[n][:, j * P : (j + 1) * P], ident_f32[:]
                    )
                move_t_of[n] = move_t

            def finish(n):
                c, t = divmod(n, COL_TILES)
                feats = slice(t * P, (t + 1) * P)
                if t == 0:
                    out_rows = work.tile([P, ROW_TILES, WIDTH], F32, bufs=2)
                    out_rows_of[c] = out_rows
                nc.vector.tensor_tensor(
                    out=out_rows_of[c][:, :, feats], in0=move_t_of[n][:],
                    in1=d_chunks[c][:, :, feats], op=ALU.add,
                )
                nc.sync.dma_start(
                    out=chunk_view(out, c)[:, :, feats], in_=out_rows_of[c][:, :, feats]
                )

            for n in range(-1, N_UNITS + 5):
                ahead = n // COL_TILES + 2
                if n % COL_TILES == 0 and DETER_BUFS <= ahead < N_CHUNKS:
                    load_deter(ahead)
                if is_unit(n):
                    reset_gate(n)
                if is_unit(n - 1):
                    candidate(n - 1)
                if is_unit(n):
                    update_gate(n)
                if is_unit(n + 1):
                    gate_product(R, n + 1)
                    gate_product(C, n + 1)
                if is_unit(n - 4):
                    transpose_move(n - 4)
                if is_unit(n - 1):
                    transpose_deter(n - 1)
                if is_unit(n + 1):
                    gate_product(Z, n + 1)
                if is_unit(n):
                    gate_candidate(n)
                if is_unit(n - 2):
                    step_towards_candidate(n - 2)
                if is_unit(n - 4):
                    finish(n - 4)
                if is_unit(n - 3):
                    scale_step(n - 3)
